import numpy as np
import ml_dtypes


def mxq(x, axis, fmt="e4m3"):
    dtype, down = {"e4m3": (ml_dtypes.float8_e4m3fn, 7), "e5m2": (ml_dtypes.float8_e5m2, 14)}[fmt]
    v = np.moveaxis(np.asarray(x, np.float32).astype(ml_dtypes.bfloat16).astype(np.float64), axis, -1)
    blocks = v.reshape(v.shape[:-1] + (-1, 32))
    amax = np.abs(blocks).max(-1, keepdims=True)
    byte = np.maximum(np.where(amax > 0, np.frexp(amax)[1] - 1 + 127, 0) - down, 1)
    scale = np.exp2(byte - 127.0)
    codes = (blocks / scale).astype(np.float32).astype(dtype).astype(np.float64)
    return np.moveaxis((codes * scale).reshape(v.shape), -1, axis)


WIDE = False


def mx_kscale(k):
    if not WIDE:
        return np.ones(k)
    levels = np.array([10, -10, 5, -5, 0])
    a = np.random.permutation(np.resize(levels, k // 512 * 4)).reshape(k // 512, 4)
    idx = np.arange(k)
    return np.exp2(a[idx // 512, idx % 128 // 32])


BF16 = ml_dtypes.bfloat16


def bf(x):
    return np.asarray(x, np.float32).astype(BF16)


def f64(x):
    return np.asarray(x).astype(np.float64)


B, L, E, H, DH, RK, RD, MAXLEN = 4, 1024, 512, 4, 64, 512, 128, 4096


def apply_rope(x, cos, sin):
    cos = cos[None, :, None, :]
    sin = sin[None, :, None, :]
    x1, x2 = x[..., 0::2], x[..., 1::2]
    out_real = x1 * cos - x2 * sin
    out_imag = x1 * sin + x2 * cos
    return np.stack([out_real, out_imag], axis=-1).reshape(x.shape)


def setup_inputs():
    s, t = mx_kscale(E), mx_kscale(RK)
    tc = np.concatenate([t, np.ones(RD)])
    return {"x": bf(np.random.standard_normal((B, L, E)) * s),
            "cos": bf(np.random.uniform(size=(L, RD // 2))),
            "sin": bf(np.random.uniform(size=(L, RD // 2))),
            "wkv_down": bf(np.random.standard_normal((E, RK + RD)) / np.sqrt(E) / s[:, None] * tc),
            "w_up": bf(np.random.standard_normal((RK, H * (2 * DH + RD))) / np.sqrt(RK) / t[:, None])}


def reference(x, cos, sin, wkv_down, w_up):
    kv_lat = mxq(f64(x), 2, "e4m3") @ mxq(f64(wkv_down), 0, "e4m3")
    c_kv = kv_lat[..., :RK]
    k_rope = kv_lat[..., RK:]
    k_rope = apply_rope(k_rope[:, :, None, :], f64(cos), f64(sin))[:, :, 0, :]
    up = (mxq(c_kv, 2, "e4m3") @ mxq(f64(w_up), 0, "e4m3")).reshape(B, L, H, 2 * DH + RD)
    k_head = up[..., :DH]
    v_head = up[..., DH:2 * DH]
    v_rope = up[..., 2 * DH:]
    k_rope_b = np.broadcast_to(k_rope[:, :, None, :], (B, L, H, RD))
    k = np.concatenate([k_head, k_rope_b], axis=-1)
    v = np.concatenate([v_head, v_rope], axis=-1)
    return k, v

@@ -1,0 +1,285 @@
+from contextlib import ExitStack
+
+import concourse.mybir as mybir
+from concourse.masks import make_identity
+
+F32 = mybir.dt.float32
+BF16 = mybir.dt.bfloat16
+U32 = mybir.dt.uint32
+U8 = mybir.dt.uint8
+FP8X4 = mybir.dt.float8_e4m3fn_x4
+MULT = mybir.AluOpType.mult
+ADD = mybir.AluOpType.add
+
+P = 128
+PACK = 4
+
+BATCH, LENGTH, EMBED = 4, 1024, 512
+HEADS, HEAD_DIM, LATENT, ROPE = 4, 64, 512, 128
+UP_HEAD = 2 * HEAD_DIM + ROPE
+OUT_HEAD = HEAD_DIM + ROPE
+OUT_ROW = HEADS * OUT_HEAD
+
+FLOPS = 2 * BATCH * LENGTH * (EMBED * (LATENT + ROPE) + LATENT * HEADS * UP_HEAD)
+
+SLOTS_PER_ROW = LENGTH // P
+SLOTS = 4
+GROUPS_PER_ROW = SLOTS_PER_ROW // SLOTS
+GROUPS = BATCH * GROUPS_PER_ROW
+GROUP_TOKENS = SLOTS * P
+PAIRS = SLOTS // 2
+WORDS = EMBED // 2
+BANK = 512
+STAGE_BUFS = 4
+
+
+def tile_multiheadlatentattention_pa_t_kernel(
+    tc, x, cos, sin, wkv_down, w_up, out_0, out_1
+):
+    nc = tc.nc
+    with ExitStack() as ctx:
+        const = ctx.enter_context(tc.tile_pool(name="const", bufs=1))
+        work = ctx.enter_context(tc.tile_pool(name="work", bufs=2))
+        psum = ctx.enter_context(tc.psum_pool(name="psum", bufs=2))
+
+        wd_raw = const.tile([P, PACK, LATENT + ROPE], BF16)
+        nc.sync.dma_start(
+            out=wd_raw[:].rearrange("p (u e) c -> p u e c", u=2),
+            in_=wkv_down.rearrange("(u p e) c -> p u e c", u=2, e=2),
+        )
+        x_view = x.rearrange("b (p i) k -> b p i k", i=SLOTS_PER_ROW)
+        x_rows = {}
+
+        def load_tokens(g):
+            row, part = divmod(g, GROUPS_PER_ROW)
+            rows = const.tile([P, SLOTS, EMBED], BF16, name="x_rows%d" % g)
+            nc.sync.dma_start(
+                out=rows[:], in_=x_view[row, :, part * SLOTS : (part + 1) * SLOTS, :]
+            )
+            x_rows[g] = rows
+
+        load_tokens(0)
+        wu_raw = const.tile([P, PACK, HEADS * UP_HEAD], BF16)
+        nc.sync.dma_start(out=wu_raw[:], in_=w_up.rearrange("(p j) n -> p j n", j=PACK))
+        load_tokens(1)
+        cos_sb = const.tile([P, SLOTS_PER_ROW, ROPE // 2], BF16)
+        nc.sync.dma_start(out=cos_sb[:], in_=cos.rearrange("(p i) j -> p i j", i=SLOTS_PER_ROW))
+        sin_sb = const.tile([P, SLOTS_PER_ROW, ROPE // 2], BF16)
+        nc.sync.dma_start(out=sin_sb[:], in_=sin.rearrange("(p i) j -> p i j", i=SLOTS_PER_ROW))
+        for g in range(2, GROUPS):
+            load_tokens(g)
+
+        ident = const.tile([P, P], F32)
+        make_identity(nc, ident[:])
+
+        wd_cols = LATENT + 2 * ROPE
+        wd_grouped = const.tile([P, wd_cols, PACK], BF16, align_bytes=64)
+        wd_codes = const.tile([P, wd_cols], U32, align_bytes=64)
+        wd_scales = const.tile([P, wd_cols], U8, align_bytes=64)
+        nc.vector.tensor_copy(
+            out=wd_grouped[:, 0:LATENT, :].rearrange("p (t m) j -> p t m j", t=PACK),
+            in_=wd_raw[:, :, 0:LATENT].rearrange("p j (m t) -> p t m j", t=PACK),
+        )
+        rope_raw = wd_raw[:, :, LATENT : LATENT + ROPE]
+        nc.vector.tensor_copy(
+            out=wd_grouped[:, LATENT : LATENT + ROPE, :],
+            in_=rope_raw.rearrange("p j c -> p c j"),
+        )
+        turned = wd_grouped[:, LATENT + ROPE : wd_cols, :].rearrange("p (q e) j -> p q e j", e=2)
+        rope_pairs = rope_raw.rearrange("p j (q e) -> p q e j", e=2)
+        nc.vector.tensor_scalar_mul(out=turned[:, :, 0, :], in0=rope_pairs[:, :, 1, :], scalar1=-1.0)
+        nc.vector.tensor_copy(out=turned[:, :, 1, :], in_=rope_pairs[:, :, 0, :])
+        for cols in (slice(0, LATENT), slice(LATENT, wd_cols)):
+            nc.vector.quantize_mx(
+                out=wd_codes[:, cols].bitcast(FP8X4),
+                scales=wd_scales[:, cols],
+                in_=wd_grouped[:, cols, :].rearrange("p c j -> p (c j)"),
+            )
+
+        wu_grouped = const.tile([P, HEADS * UP_HEAD, PACK], BF16, align_bytes=64)
+        wu_codes = const.tile([P, HEADS * UP_HEAD], U32, align_bytes=64)
+        wu_scales = const.tile([P, HEADS * UP_HEAD], U8, align_bytes=64)
+
+        def regroup_w_up(half):
+            cols = slice(half * BANK, (half + 1) * BANK)
+            nc.scalar.copy(
+                out=wu_grouped[:, cols, :], in_=wu_raw[:, :, cols].rearrange("p j c -> p c j")
+            )
+
+        def quantise_w_up(half):
+            cols = slice(half * BANK, (half + 1) * BANK)
+            nc.vector.quantize_mx(
+                out=wu_codes[:, cols].bitcast(FP8X4),
+                scales=wu_scales[:, cols],
+                in_=wu_grouped[:, cols, :].rearrange("p c j -> p (c j)"),
+            )
+
+        x_grouped = {}
+        x_mx = {}
+        c_grouped = {}
+        c_mx = {}
+        products = {}
+        k_stage = {}
+        v_stage = {}
+
+        def transpose_tokens(g):
+            words = x_rows[g][:].rearrange("p i k -> p (i k)").bitcast(F32)
+            grouped = work.tile([P, GROUP_TOKENS * PACK], BF16, tag="x_grouped", align_bytes=64)
+            grouped_words = grouped[:].bitcast(F32).rearrange("p (i n u) -> p i n u", i=SLOTS, u=2)
+            for pair in range(PAIRS):
+                xt = psum.tile([P, 2, 2, P], F32, tag="xt", bufs=2)
+                for s in range(2):
+                    for u in range(2):
+                        first = (2 * pair + s) * WORDS + u * P
+                        nc.tensor.transpose(xt[:, s, u, :], words[:, first : first + P], ident[:])
+                nc.scalar.copy(
+                    out=grouped_words[:, 2 * pair : 2 * pair + 2, :, :],
+                    in_=xt[:].rearrange("p s u n -> p s n u"),
+                )
+            x_grouped[g] = grouped
+
+        def quantise_tokens(g):
+            codes = work.tile([P, GROUP_TOKENS], U32, tag="x_codes", bufs=3, align_bytes=64)
+            scales = work.tile([P, GROUP_TOKENS], U8, tag="x_scales", bufs=3, align_bytes=64)
+            nc.vector.quantize_mx(out=codes[:].bitcast(FP8X4), scales=scales[:], in_=x_grouped[g][:])
+            x_mx[g] = (codes, scales)
+
+        def latent_slot(g, i):
+            if i == 0:
+                c_grouped[g] = work.tile(
+                    [P, GROUP_TOKENS, PACK], BF16, tag="c_grouped", name="c_grouped", align_bytes=64
+                )
+            codes, scales = x_mx[g]
+            tokens = slice(i * P, (i + 1) * P)
+            c_ps = psum.tile([P, PACK, P], F32, tag="c", bufs=2)
+            for t in range(PACK):
+                block = slice(t * P, (t + 1) * P)
+                nc.tensor.matmul_mx(
+                    out=c_ps[:, t, :],
+                    lhsT=wd_codes[:, block].bitcast(FP8X4),
+                    lhsT_scale=wd_scales[:, block],
+                    rhs=codes[:, tokens].bitcast(FP8X4),
+                    rhs_scale=scales[:, tokens],
+                    start=True,
+                    stop=True,
+                )
+            nc.vector.tensor_copy(
+                out=c_grouped[g][:, tokens, :], in_=c_ps[:].rearrange("p t n -> p n t")
+            )
+
+        def quantise_latent(g):
+            codes = work.tile([P, GROUP_TOKENS], U32, tag="c_codes", align_bytes=64)
+            scales = work.tile([P, GROUP_TOKENS], U8, tag="c_scales", align_bytes=64)
+            nc.vector.quantize_mx(
+                out=codes[:].bitcast(FP8X4),
+                scales=scales[:],
+                in_=c_grouped[g][:].rearrange("p n t -> p (n t)"),
+            )
+            c_mx[g] = (codes, scales)
+
+        def open_stage(g):
+            k_stage[g] = work.tile(
+                [P, SLOTS, HEADS, OUT_HEAD], F32, tag="k_stage", name="k_stage", bufs=STAGE_BUFS
+            )
+            v_stage[g] = work.tile(
+                [P, SLOTS, HEADS, OUT_HEAD], F32, tag="v_stage", name="v_stage", bufs=STAGE_BUFS
+            )
+            products[g] = work.tile([P, 2, SLOTS, ROPE], F32, tag="products", name="products")
+
+        def up_slot(g, i):
+            codes, scales = c_mx[g]
+            tokens = slice(i * P, (i + 1) * P)
+            for half in range(2):
+                cols = slice(half * BANK, (half + 1) * BANK)
+                heads = slice(2 * half, 2 * half + 2)
+                up_ps = psum.tile([P, 2, UP_HEAD], F32, tag="up", bufs=3)
+                nc.tensor.matmul_mx(
+                    out=up_ps[:].rearrange("p h c -> p (h c)"),
+                    lhsT=codes[:, tokens].bitcast(FP8X4),
+                    lhsT_scale=scales[:, tokens],
+                    rhs=wu_codes[:, cols].bitcast(FP8X4),
+                    rhs_scale=wu_scales[:, cols],
+                    start=True,
+                    stop=True,
+                )
+                nc.scalar.copy(out=k_stage[g][:, i, heads, 0:HEAD_DIM], in_=up_ps[:, :, 0:HEAD_DIM])
+                nc.scalar.copy(out=v_stage[g][:, i, heads, :], in_=up_ps[:, :, HEAD_DIM:UP_HEAD])
+
+        def rope_pair(g, pair):
+            codes, scales = x_mx[g]
+            cols = slice(LATENT, wd_cols)
+            r_ps = psum.tile([P, 2, 2, ROPE], F32, tag="r", bufs=1)
+            for s in range(2):
+                tokens = slice((2 * pair + s) * P, (2 * pair + s + 1) * P)
+                nc.tensor.matmul_mx(
+                    out=r_ps[:, s, :, :].rearrange("p w c -> p (w c)"),
+                    lhsT=codes[:, tokens].bitcast(FP8X4),
+                    lhsT_scale=scales[:, tokens],
+                    rhs=wd_codes[:, cols].bitcast(FP8X4),
+                    rhs_scale=wd_scales[:, cols],
+                    start=True,
+                    stop=True,
+                )
+            first = (g % GROUPS_PER_ROW) * SLOTS + 2 * pair
+            for w, table in enumerate((cos_sb, sin_sb)):
+                nc.vector.tensor_tensor(
+                    out=products[g][:, w, 2 * pair : 2 * pair + 2, :].rearrange(
+                        "p s (q e) -> p s q e", e=2
+                    ),
+                    in0=r_ps[:, :, w, :].rearrange("p s (q e) -> p s q e", e=2),
+                    in1=table[:, first : first + 2, :].unsqueeze(3).to_broadcast([P, 2, ROPE // 2, 2]),
+                    op=MULT,
+                )
+
+        def rope_sum(g):
+            nc.vector.tensor_tensor(
+                out=k_stage[g][:, :, 0, HEAD_DIM:OUT_HEAD],
+                in0=products[g][:, 0, :, :],
+                in1=products[g][:, 1, :, :],
+                op=ADD,
+            )
+
+        def rope_spread(g):
+            nc.vector.tensor_copy(
+                out=k_stage[g][:, :, 1:HEADS, HEAD_DIM:OUT_HEAD],
+                in_=k_stage[g][:, :, 0:1, HEAD_DIM:OUT_HEAD].to_broadcast([P, SLOTS, HEADS - 1, ROPE]),
+            )
+
+        k_view = out_0.rearrange("b (p i) h d -> b p i h d", i=SLOTS_PER_ROW)
+        v_view = out_1.rearrange("b (p i) h d -> b p i h d", i=SLOTS_PER_ROW)
+
+        def store(g):
+            row, part = divmod(g, GROUPS_PER_ROW)
+            slots = slice(part * SLOTS, (part + 1) * SLOTS)
+            nc.sync.dma_start(out=v_view[row, :, slots, :, :], in_=v_stage[g][:])
+            nc.sync.dma_start(out=k_view[row, :, slots, :, :], in_=k_stage[g][:])
+
+        transpose_tokens(0)
+        regroup_w_up(0)
+        quantise_tokens(0)
+        transpose_tokens(1)
+        regroup_w_up(1)
+        for i in range(SLOTS):
+            latent_slot(0, i)
+        quantise_tokens(1)
+        quantise_w_up(0)
+        quantise_latent(0)
+        quantise_w_up(1)
+
+        for g in range(GROUPS):
+            open_stage(g)
+            if g + 2 < GROUPS:
+                transpose_tokens(g + 2)
+            for i in range(SLOTS):
+                if g + 1 < GROUPS:
+                    latent_slot(g + 1, i)
+                up_slot(g, i)
+                if i < PAIRS:
+                    rope_pair(g, i)
+            rope_sum(g)
+            if g + 2 < GROUPS:
+                quantise_tokens(g + 2)
+            rope_spread(g)
+            if g + 1 < GROUPS:
+                quantise_latent(g + 1)
+            store(g)

@@ -18,19 +18,20 @@ BATCH, LENGTH, EMBED = 4, 1024, 512
 HEADS, HEAD_DIM, LATENT, ROPE = 4, 64, 512, 128
 UP_HEAD = 2 * HEAD_DIM + ROPE
 OUT_HEAD = HEAD_DIM + ROPE
-OUT_ROW = HEADS * OUT_HEAD
 
 FLOPS = 2 * BATCH * LENGTH * (EMBED * (LATENT + ROPE) + LATENT * HEADS * UP_HEAD)
 
 SLOTS_PER_ROW = LENGTH // P
+PAIR = 2
 SLOTS = 4
-GROUPS_PER_ROW = SLOTS_PER_ROW // SLOTS
-GROUPS = BATCH * GROUPS_PER_ROW
-GROUP_TOKENS = SLOTS * P
-PAIRS = SLOTS // 2
+ALL_SLOTS = BATCH * SLOTS_PER_ROW
+SIZES = (PAIR, PAIR) + (SLOTS,) * (ALL_SLOTS // SLOTS - 1)
+GROUPS = len(SIZES)
+STARTS = tuple(sum(SIZES[:g]) for g in range(GROUPS))
+LOADS = ALL_SLOTS // SLOTS
 WORDS = EMBED // 2
 BANK = 512
-STAGE_BUFS = 4
+STAGE_BUFS = 8
 
 
 def tile_multiheadlatentattention_pa_t_kernel(
@@ -41,6 +42,7 @@ def tile_multiheadlatentattention_pa_t_kernel(
         const = ctx.enter_context(tc.tile_pool(name="const", bufs=1))
         work = ctx.enter_context(tc.tile_pool(name="work", bufs=2))
         psum = ctx.enter_context(tc.psum_pool(name="psum", bufs=2))
+        ctx.enter_context(tc.manual_schedule())
 
         wd_raw = const.tile([P, PACK, LATENT + ROPE], BF16)
         nc.sync.dma_start(
@@ -50,24 +52,21 @@ def tile_multiheadlatentattention_pa_t_kernel(
         x_view = x.rearrange("b (p i) k -> b p i k", i=SLOTS_PER_ROW)
         x_rows = {}
 
-        def load_tokens(g):
-            row, part = divmod(g, GROUPS_PER_ROW)
-            rows = const.tile([P, SLOTS, EMBED], BF16, name="x_rows%d" % g)
-            nc.sync.dma_start(
-                out=rows[:], in_=x_view[row, :, part * SLOTS : (part + 1) * SLOTS, :]
-            )
-            x_rows[g] = rows
+        def load_tokens(n):
+            row, first = divmod(n * SLOTS, SLOTS_PER_ROW)
+            rows = const.tile([P, SLOTS, EMBED], BF16, name="x_rows%d" % n)
+            nc.sync.dma_start(out=rows[:], in_=x_view[row, :, first : first + SLOTS, :])
+            x_rows[n] = rows
 
         load_tokens(0)
         wu_raw = const.tile([P, PACK, HEADS * UP_HEAD], BF16)
         nc.sync.dma_start(out=wu_raw[:], in_=w_up.rearrange("(p j) n -> p j n", j=PACK))
-        load_tokens(1)
         cos_sb = const.tile([P, SLOTS_PER_ROW, ROPE // 2], BF16)
         nc.sync.dma_start(out=cos_sb[:], in_=cos.rearrange("(p i) j -> p i j", i=SLOTS_PER_ROW))
         sin_sb = const.tile([P, SLOTS_PER_ROW, ROPE // 2], BF16)
         nc.sync.dma_start(out=sin_sb[:], in_=sin.rearrange("(p i) j -> p i j", i=SLOTS_PER_ROW))
-        for g in range(2, GROUPS):
-            load_tokens(g)
+        for n in range(1, LOADS):
+            load_tokens(n)
 
         ident = const.tile([P, P], F32)
         make_identity(nc, ident[:])
@@ -76,20 +75,27 @@ def tile_multiheadlatentattention_pa_t_kernel(
         wd_grouped = const.tile([P, wd_cols, PACK], BF16, align_bytes=64)
         wd_codes = const.tile([P, wd_cols], U32, align_bytes=64)
         wd_scales = const.tile([P, wd_cols], U8, align_bytes=64)
-        nc.vector.tensor_copy(
-            out=wd_grouped[:, 0:LATENT, :].rearrange("p (t m) j -> p t m j", t=PACK),
-            in_=wd_raw[:, :, 0:LATENT].rearrange("p j (m t) -> p t m j", t=PACK),
-        )
-        rope_raw = wd_raw[:, :, LATENT : LATENT + ROPE]
-        nc.vector.tensor_copy(
-            out=wd_grouped[:, LATENT : LATENT + ROPE, :],
-            in_=rope_raw.rearrange("p j c -> p c j"),
-        )
-        turned = wd_grouped[:, LATENT + ROPE : wd_cols, :].rearrange("p (q e) j -> p q e j", e=2)
-        rope_pairs = rope_raw.rearrange("p j (q e) -> p q e j", e=2)
-        nc.vector.tensor_scalar_mul(out=turned[:, :, 0, :], in0=rope_pairs[:, :, 1, :], scalar1=-1.0)
-        nc.vector.tensor_copy(out=turned[:, :, 1, :], in_=rope_pairs[:, :, 0, :])
-        for cols in (slice(0, LATENT), slice(LATENT, wd_cols)):
+
+        def regroup_latent_weights():
+            nc.vector.tensor_copy(
+                out=wd_grouped[:, 0:LATENT, :].rearrange("p (t m) j -> p t m j", t=PACK),
+                in_=wd_raw[:, :, 0:LATENT].rearrange("p j (m t) -> p t m j", t=PACK),
+            )
+
+        def regroup_rope_weights():
+            rope_raw = wd_raw[:, :, LATENT : LATENT + ROPE]
+            nc.scalar.copy(
+                out=wd_grouped[:, LATENT : LATENT + ROPE, :],
+                in_=rope_raw.rearrange("p j c -> p c j"),
+            )
+            turned = wd_grouped[:, LATENT + ROPE : wd_cols, :].rearrange(
+                "p (q e) j -> p q e j", e=2
+            )
+            rope_pairs = rope_raw.rearrange("p j (q e) -> p q e j", e=2)
+            nc.scalar.mul(out=turned[:, :, 0, :], in_=rope_pairs[:, :, 1, :], mul=-1.0)
+            nc.scalar.copy(out=turned[:, :, 1, :], in_=rope_pairs[:, :, 0, :])
+
+        def quantise_wkv_down(cols):
             nc.vector.quantize_mx(
                 out=wd_codes[:, cols].bitcast(FP8X4),
                 scales=wd_scales[:, cols],
@@ -100,11 +106,9 @@ def tile_multiheadlatentattention_pa_t_kernel(
         wu_codes = const.tile([P, HEADS * UP_HEAD], U32, align_bytes=64)
         wu_scales = const.tile([P, HEADS * UP_HEAD], U8, align_bytes=64)
 
-        def regroup_w_up(half):
+        def regroup_w_up(half, copy):
             cols = slice(half * BANK, (half + 1) * BANK)
-            nc.scalar.copy(
-                out=wu_grouped[:, cols, :], in_=wu_raw[:, :, cols].rearrange("p j c -> p c j")
-            )
+            copy(out=wu_grouped[:, cols, :], in_=wu_raw[:, :, cols].rearrange("p j c -> p c j"))
 
         def quantise_w_up(half):
             cols = slice(half * BANK, (half + 1) * BANK)
@@ -118,36 +122,37 @@ def tile_multiheadlatentattention_pa_t_kernel(
         x_mx = {}
         c_grouped = {}
         c_mx = {}
-        products = {}
         k_stage = {}
         v_stage = {}
 
         def transpose_tokens(g):
-            words = x_rows[g][:].rearrange("p i k -> p (i k)").bitcast(F32)
-            grouped = work.tile([P, GROUP_TOKENS * PACK], BF16, tag="x_grouped", align_bytes=64)
-            grouped_words = grouped[:].bitcast(F32).rearrange("p (i n u) -> p i n u", i=SLOTS, u=2)
-            for pair in range(PAIRS):
-                xt = psum.tile([P, 2, 2, P], F32, tag="xt", bufs=2)
-                for s in range(2):
+            load, local = divmod(STARTS[g], SLOTS)
+            words = x_rows[load][:].rearrange("p i k -> p (i k)").bitcast(F32)
+            grouped = work.tile([P, SIZES[g] * P * PACK], BF16, tag="x_grouped", align_bytes=64)
+            grouped_words = grouped[:].bitcast(F32).rearrange("p (i n u) -> p i n u", n=P, u=2)
+            for i in range(0, SIZES[g], PAIR):
+                xt = psum.tile([P, PAIR, 2, P], F32, tag="xt", bufs=2)
+                for s in range(PAIR):
                     for u in range(2):
-                        first = (2 * pair + s) * WORDS + u * P
+                        first = (local + i + s) * WORDS + u * P
                         nc.tensor.transpose(xt[:, s, u, :], words[:, first : first + P], ident[:])
-                nc.scalar.copy(
-                    out=grouped_words[:, 2 * pair : 2 * pair + 2, :, :],
+                copy = nc.scalar.copy if i == 0 else nc.vector.tensor_copy
+                copy(
+                    out=grouped_words[:, i : i + PAIR, :, :],
                     in_=xt[:].rearrange("p s u n -> p s n u"),
                 )
             x_grouped[g] = grouped
 
         def quantise_tokens(g):
-            codes = work.tile([P, GROUP_TOKENS], U32, tag="x_codes", bufs=3, align_bytes=64)
-            scales = work.tile([P, GROUP_TOKENS], U8, tag="x_scales", bufs=3, align_bytes=64)
+            codes = work.tile([P, SIZES[g] * P], U32, tag="x_codes", bufs=3, align_bytes=64)
+            scales = work.tile([P, SIZES[g] * P], U8, tag="x_scales", bufs=3, align_bytes=64)
             nc.vector.quantize_mx(out=codes[:].bitcast(FP8X4), scales=scales[:], in_=x_grouped[g][:])
             x_mx[g] = (codes, scales)
 
         def latent_slot(g, i):
             if i == 0:
                 c_grouped[g] = work.tile(
-                    [P, GROUP_TOKENS, PACK], BF16, tag="c_grouped", name="c_grouped", align_bytes=64
+                    [P, SIZES[g] * P, PACK], BF16, tag="c_grouped", name="c_grouped", align_bytes=64
                 )
             codes, scales = x_mx[g]
             tokens = slice(i * P, (i + 1) * P)
@@ -168,8 +173,8 @@ def tile_multiheadlatentattention_pa_t_kernel(
             )
 
         def quantise_latent(g):
-            codes = work.tile([P, GROUP_TOKENS], U32, tag="c_codes", align_bytes=64)
-            scales = work.tile([P, GROUP_TOKENS], U8, tag="c_scales", align_bytes=64)
+            codes = work.tile([P, SIZES[g] * P], U32, tag="c_codes", align_bytes=64)
+            scales = work.tile([P, SIZES[g] * P], U8, tag="c_scales", align_bytes=64)
             nc.vector.quantize_mx(
                 out=codes[:].bitcast(FP8X4),
                 scales=scales[:],
@@ -177,18 +182,54 @@ def tile_multiheadlatentattention_pa_t_kernel(
             )
             c_mx[g] = (codes, scales)
 
-        def open_stage(g):
-            k_stage[g] = work.tile(
-                [P, SLOTS, HEADS, OUT_HEAD], F32, tag="k_stage", name="k_stage", bufs=STAGE_BUFS
+        def rope_pair(g, i):
+            shape = [P, PAIR, HEADS, OUT_HEAD]
+            k_rows = work.tile(shape, F32, tag="k_stage", bufs=STAGE_BUFS)
+            v_rows = work.tile(shape, F32, tag="v_stage", bufs=STAGE_BUFS)
+            k_stage[g, i] = k_rows
+            v_stage[g, i] = v_rows
+            codes, scales = x_mx[g]
+            cols = slice(LATENT, wd_cols)
+            r_ps = psum.tile([P, PAIR, 2, ROPE], F32, tag="r", bufs=1)
+            for s in range(PAIR):
+                tokens = slice((i + s) * P, (i + s + 1) * P)
+                nc.tensor.matmul_mx(
+                    out=r_ps[:, s, :, :].rearrange("p w c -> p (w c)"),
+                    lhsT=codes[:, tokens].bitcast(FP8X4),
+                    lhsT_scale=scales[:, tokens],
+                    rhs=wd_codes[:, cols].bitcast(FP8X4),
+                    rhs_scale=wd_scales[:, cols],
+                    start=True,
+                    stop=True,
+                )
+            first = STARTS[g] % SLOTS_PER_ROW + i
+            terms = work.tile([P, 2, PAIR, ROPE], F32, tag="terms", bufs=3)
+            for w, table in enumerate((cos_sb, sin_sb)):
+                nc.vector.tensor_tensor(
+                    out=terms[:, w, :, :].rearrange("p s (q e) -> p s q e", e=2),
+                    in0=r_ps[:, :, w, :].rearrange("p s (q e) -> p s q e", e=2),
+                    in1=table[:, first : first + PAIR, :]
+                    .unsqueeze(3)
+                    .to_broadcast([P, PAIR, ROPE // 2, 2]),
+                    op=MULT,
+                )
+            nc.gpsimd.tensor_tensor(
+                out=k_rows[:, :, 0, HEAD_DIM:OUT_HEAD], in0=terms[:, 0, :, :], in1=terms[:, 1, :, :], op=ADD
             )
-            v_stage[g] = work.tile(
-                [P, SLOTS, HEADS, OUT_HEAD], F32, tag="v_stage", name="v_stage", bufs=STAGE_BUFS
+            nc.gpsimd.tensor_scalar(
+                out=k_rows[:, :, 1:HEADS, HEAD_DIM:OUT_HEAD],
+                in0=k_rows[:, :, 0:1, HEAD_DIM:OUT_HEAD].to_broadcast([P, PAIR, HEADS - 1, ROPE]),
+                scalar1=1.0,
+                scalar2=0.0,
+                op0=MULT,
+                op1=ADD,
             )
-            products[g] = work.tile([P, 2, SLOTS, ROPE], F32, tag="products", name="products")
 
         def up_slot(g, i):
             codes, scales = c_mx[g]
             tokens = slice(i * P, (i + 1) * P)
+            k_rows = k_stage[g, i - i % PAIR]
+            v_rows = v_stage[g, i - i % PAIR]
             for half in range(2):
                 cols = slice(half * BANK, (half + 1) * BANK)
                 heads = slice(2 * half, 2 * half + 2)
@@ -202,84 +243,47 @@ def tile_multiheadlatentattention_pa_t_kernel(
                     start=True,
                     stop=True,
                 )
-                nc.scalar.copy(out=k_stage[g][:, i, heads, 0:HEAD_DIM], in_=up_ps[:, :, 0:HEAD_DIM])
-                nc.scalar.copy(out=v_stage[g][:, i, heads, :], in_=up_ps[:, :, HEAD_DIM:UP_HEAD])
-
-        def rope_pair(g, pair):
-            codes, scales = x_mx[g]
-            cols = slice(LATENT, wd_cols)
-            r_ps = psum.tile([P, 2, 2, ROPE], F32, tag="r", bufs=1)
-            for s in range(2):
-                tokens = slice((2 * pair + s) * P, (2 * pair + s + 1) * P)
-                nc.tensor.matmul_mx(
-                    out=r_ps[:, s, :, :].rearrange("p w c -> p (w c)"),
-                    lhsT=codes[:, tokens].bitcast(FP8X4),
-                    lhsT_scale=scales[:, tokens],
-                    rhs=wd_codes[:, cols].bitcast(FP8X4),
-                    rhs_scale=wd_scales[:, cols],
-                    start=True,
-                    stop=True,
-                )
-            first = (g % GROUPS_PER_ROW) * SLOTS + 2 * pair
-            for w, table in enumerate((cos_sb, sin_sb)):
-                nc.vector.tensor_tensor(
-                    out=products[g][:, w, 2 * pair : 2 * pair + 2, :].rearrange(
-                        "p s (q e) -> p s q e", e=2
-                    ),
-                    in0=r_ps[:, :, w, :].rearrange("p s (q e) -> p s q e", e=2),
-                    in1=table[:, first : first + 2, :].unsqueeze(3).to_broadcast([P, 2, ROPE // 2, 2]),
-                    op=MULT,
-                )
-
-        def rope_sum(g):
-            nc.vector.tensor_tensor(
-                out=k_stage[g][:, :, 0, HEAD_DIM:OUT_HEAD],
-                in0=products[g][:, 0, :, :],
-                in1=products[g][:, 1, :, :],
-                op=ADD,
-            )
-
-        def rope_spread(g):
-            nc.vector.tensor_copy(
-                out=k_stage[g][:, :, 1:HEADS, HEAD_DIM:OUT_HEAD],
-                in_=k_stage[g][:, :, 0:1, HEAD_DIM:OUT_HEAD].to_broadcast([P, SLOTS, HEADS - 1, ROPE]),
-            )
+                nc.scalar.copy(out=k_rows[:, i % PAIR, heads, 0:HEAD_DIM], in_=up_ps[:, :, 0:HEAD_DIM])
+                nc.scalar.copy(out=v_rows[:, i % PAIR, heads, :], in_=up_ps[:, :, HEAD_DIM:UP_HEAD])
 
         k_view = out_0.rearrange("b (p i) h d -> b p i h d", i=SLOTS_PER_ROW)
         v_view = out_1.rearrange("b (p i) h d -> b p i h d", i=SLOTS_PER_ROW)
 
-        def store(g):
-            row, part = divmod(g, GROUPS_PER_ROW)
-            slots = slice(part * SLOTS, (part + 1) * SLOTS)
-            nc.sync.dma_start(out=v_view[row, :, slots, :, :], in_=v_stage[g][:])
-            nc.sync.dma_start(out=k_view[row, :, slots, :, :], in_=k_stage[g][:])
+        def store_pair(g, i):
+            row, first = divmod(STARTS[g] + i, SLOTS_PER_ROW)
+            slots = slice(first, first + PAIR)
+            nc.sync.dma_start(out=v_view[row, :, slots, :, :], in_=v_stage[g, i][:])
+            nc.sync.dma_start(out=k_view[row, :, slots, :, :], in_=k_stage[g, i][:])
 
+        regroup_latent_weights()
+        regroup_rope_weights()
         transpose_tokens(0)
-        regroup_w_up(0)
-        quantise_tokens(0)
         transpose_tokens(1)
-        regroup_w_up(1)
-        for i in range(SLOTS):
-            latent_slot(0, i)
+        quantise_wkv_down(slice(0, LATENT))
+        quantise_tokens(0)
+        quantise_wkv_down(slice(LATENT, wd_cols))
         quantise_tokens(1)
-        quantise_w_up(0)
+        for i in range(SIZES[0]):
+            latent_slot(0, i)
+        regroup_w_up(0, nc.scalar.copy)
+        regroup_w_up(1, nc.vector.tensor_copy)
         quantise_latent(0)
         quantise_w_up(1)
+        quantise_w_up(0)
 
         for g in range(GROUPS):
-            open_stage(g)
             if g + 2 < GROUPS:
                 transpose_tokens(g + 2)
             for i in range(SLOTS):
-                if g + 1 < GROUPS:
-                    latent_slot(g + 1, i)
-                up_slot(g, i)
-                if i < PAIRS:
+                if i < SIZES[g] and i % PAIR == 0:
                     rope_pair(g, i)
-            rope_sum(g)
+                if g + 1 < GROUPS and i < SIZES[g + 1]:
+                    latent_slot(g + 1, i)
+                if i < SIZES[g]:
+                    up_slot(g, i)
+                    if i % PAIR == 1:
+                        store_pair(g, i - 1)
             if g + 2 < GROUPS:
                 quantise_tokens(g + 2)
-            rope_spread(g)
             if g + 1 < GROUPS:
                 quantise_latent(g + 1)
-            store(g)

@@ -23,15 +23,17 @@ FLOPS = 2 * BATCH * LENGTH * (EMBED * (LATENT + ROPE) + LATENT * HEADS * UP_HEAD
 
 SLOTS_PER_ROW = LENGTH // P
 PAIR = 2
-SLOTS = 4
+SLOTS = 2
 ALL_SLOTS = BATCH * SLOTS_PER_ROW
-SIZES = (PAIR, PAIR) + (SLOTS,) * (ALL_SLOTS // SLOTS - 1)
+SIZES = (SLOTS,) * (ALL_SLOTS // SLOTS)
 GROUPS = len(SIZES)
 STARTS = tuple(sum(SIZES[:g]) for g in range(GROUPS))
-LOADS = ALL_SLOTS // SLOTS
+LOAD_SLOTS = 4
+LOADS = ALL_SLOTS // LOAD_SLOTS
 WORDS = EMBED // 2
 BANK = 512
 STAGE_BUFS = 8
+LEAD = 1
 
 
 def tile_multiheadlatentattention_pa_t_kernel(
@@ -53,14 +55,18 @@ def tile_multiheadlatentattention_pa_t_kernel(
         x_rows = {}
 
         def load_tokens(n):
-            row, first = divmod(n * SLOTS, SLOTS_PER_ROW)
-            rows = const.tile([P, SLOTS, EMBED], BF16, name="x_rows%d" % n)
-            nc.sync.dma_start(out=rows[:], in_=x_view[row, :, first : first + SLOTS, :])
+            row, first = divmod(n * LOAD_SLOTS, SLOTS_PER_ROW)
+            rows = const.tile([P, LOAD_SLOTS, EMBED], BF16, name="x_rows%d" % n)
+            nc.sync.dma_start(out=rows[:], in_=x_view[row, :, first : first + LOAD_SLOTS, :])
             x_rows[n] = rows
 
         load_tokens(0)
-        wu_raw = const.tile([P, PACK, HEADS * UP_HEAD], BF16)
-        nc.sync.dma_start(out=wu_raw[:], in_=w_up.rearrange("(p j) n -> p j n", j=PACK))
+        wu_view = w_up.rearrange("(p j) n -> p j n", j=PACK)
+        wu_raw = []
+        for half in range(2):
+            raw = const.tile([P, PACK, BANK], BF16, name="wu_raw%d" % half)
+            nc.sync.dma_start(out=raw[:], in_=wu_view[:, :, half * BANK : (half + 1) * BANK])
+            wu_raw.append(raw)
         cos_sb = const.tile([P, SLOTS_PER_ROW, ROPE // 2], BF16)
         nc.sync.dma_start(out=cos_sb[:], in_=cos.rearrange("(p i) j -> p i j", i=SLOTS_PER_ROW))
         sin_sb = const.tile([P, SLOTS_PER_ROW, ROPE // 2], BF16)
@@ -108,7 +114,7 @@ def tile_multiheadlatentattention_pa_t_kernel(
 
         def regroup_w_up(half, copy):
             cols = slice(half * BANK, (half + 1) * BANK)
-            copy(out=wu_grouped[:, cols, :], in_=wu_raw[:, :, cols].rearrange("p j c -> p c j"))
+            copy(out=wu_grouped[:, cols, :], in_=wu_raw[half][:].rearrange("p j c -> p c j"))
 
         def quantise_w_up(half):
             cols = slice(half * BANK, (half + 1) * BANK)
@@ -126,7 +132,7 @@ def tile_multiheadlatentattention_pa_t_kernel(
         v_stage = {}
 
         def transpose_tokens(g):
-            load, local = divmod(STARTS[g], SLOTS)
+            load, local = divmod(STARTS[g], LOAD_SLOTS)
             words = x_rows[load][:].rearrange("p i k -> p (i k)").bitcast(F32)
             grouped = work.tile([P, SIZES[g] * P * PACK], BF16, tag="x_grouped", align_bytes=64)
             grouped_words = grouped[:].bitcast(F32).rearrange("p (i n u) -> p i n u", n=P, u=2)
@@ -136,7 +142,7 @@ def tile_multiheadlatentattention_pa_t_kernel(
                     for u in range(2):
                         first = (local + i + s) * WORDS + u * P
                         nc.tensor.transpose(xt[:, s, u, :], words[:, first : first + P], ident[:])
-                copy = nc.scalar.copy if i == 0 else nc.vector.tensor_copy
+                copy = nc.scalar.copy if g % 2 == 0 else nc.vector.tensor_copy
                 copy(
                     out=grouped_words[:, i : i + PAIR, :, :],
                     in_=xt[:].rearrange("p s u n -> p s n u"),
@@ -182,12 +188,13 @@ def tile_multiheadlatentattention_pa_t_kernel(
             )
             c_mx[g] = (codes, scales)
 
-        def rope_pair(g, i):
+        def open_pair(g, i):
             shape = [P, PAIR, HEADS, OUT_HEAD]
-            k_rows = work.tile(shape, F32, tag="k_stage", bufs=STAGE_BUFS)
-            v_rows = work.tile(shape, F32, tag="v_stage", bufs=STAGE_BUFS)
-            k_stage[g, i] = k_rows
-            v_stage[g, i] = v_rows
+            k_stage[g, i] = work.tile(shape, F32, tag="k_stage", name="k_stage", bufs=STAGE_BUFS)
+            v_stage[g, i] = work.tile(shape, F32, tag="v_stage", name="v_stage", bufs=STAGE_BUFS)
+
+        def rope_pair(g, i):
+            k_rows = k_stage[g, i]
             codes, scales = x_mx[g]
             cols = slice(LATENT, wd_cols)
             r_ps = psum.tile([P, PAIR, 2, ROPE], F32, tag="r", bufs=1)
@@ -255,35 +262,34 @@ def tile_multiheadlatentattention_pa_t_kernel(
             nc.sync.dma_start(out=v_view[row, :, slots, :, :], in_=v_stage[g, i][:])
             nc.sync.dma_start(out=k_view[row, :, slots, :, :], in_=k_stage[g, i][:])
 
-        regroup_latent_weights()
-        regroup_rope_weights()
-        transpose_tokens(0)
-        transpose_tokens(1)
-        quantise_wkv_down(slice(0, LATENT))
-        quantise_tokens(0)
-        quantise_wkv_down(slice(LATENT, wd_cols))
-        quantise_tokens(1)
-        for i in range(SIZES[0]):
-            latent_slot(0, i)
-        regroup_w_up(0, nc.scalar.copy)
-        regroup_w_up(1, nc.vector.tensor_copy)
-        quantise_latent(0)
-        quantise_w_up(1)
-        quantise_w_up(0)
-
-        for g in range(GROUPS):
-            if g + 2 < GROUPS:
+        def pipeline_round(g):
+            if 0 <= g + 2 < GROUPS:
                 transpose_tokens(g + 2)
-            for i in range(SLOTS):
-                if i < SIZES[g] and i % PAIR == 0:
-                    rope_pair(g, i)
-                if g + 1 < GROUPS and i < SIZES[g + 1]:
-                    latent_slot(g + 1, i)
-                if i < SIZES[g]:
+            for step in range(SLOTS + LEAD):
+                if 0 <= g + 1 < GROUPS and step < SIZES[g + 1]:
+                    latent_slot(g + 1, step)
+                i = step - LEAD
+                if 0 <= g and 0 <= i < SIZES[g]:
+                    if i % PAIR == 0:
+                        open_pair(g, i)
+                        rope_pair(g, i)
                     up_slot(g, i)
                     if i % PAIR == 1:
                         store_pair(g, i - 1)
-            if g + 2 < GROUPS:
-                quantise_tokens(g + 2)
-            if g + 1 < GROUPS:
-                quantise_latent(g + 1)
+                if step == LEAD and 0 <= g + 2 < GROUPS:
+                    quantise_tokens(g + 2)
+                if 0 <= g + 1 < GROUPS and step == SIZES[g + 1]:
+                    quantise_latent(g + 1)
+
+        regroup_latent_weights()
+        regroup_rope_weights()
+        quantise_wkv_down(slice(0, LATENT))
+        pipeline_round(-2)
+        regroup_w_up(0, nc.vector.tensor_copy)
+        regroup_w_up(1, nc.scalar.copy)
+        pipeline_round(-1)
+        quantise_w_up(0)
+        quantise_w_up(1)
+        quantise_wkv_down(slice(LATENT, wd_cols))
+        for g in range(GROUPS):
+            pipeline_round(g)

@@ -46,11 +46,10 @@ def tile_multiheadlatentattention_pa_t_kernel(
         psum = ctx.enter_context(tc.psum_pool(name="psum", bufs=2))
         ctx.enter_context(tc.manual_schedule())
 
-        wd_raw = const.tile([P, PACK, LATENT + ROPE], BF16)
-        nc.sync.dma_start(
-            out=wd_raw[:].rearrange("p (u e) c -> p u e c", u=2),
-            in_=wkv_down.rearrange("(u p e) c -> p u e c", u=2, e=2),
-        )
+        wd_view = wkv_down.rearrange("(u p e) c -> p u e c", u=2, e=2)
+        latent_raw = const.tile([P, PACK, LATENT], BF16)
+        for u in range(2):
+            nc.sync.dma_start(out=latent_raw[:, 2 * u : 2 * u + 2, :], in_=wd_view[:, u, :, 0:LATENT])
         x_view = x.rearrange("b (p i) k -> b p i k", i=SLOTS_PER_ROW)
         x_rows = {}
 
@@ -61,6 +60,11 @@ def tile_multiheadlatentattention_pa_t_kernel(
             x_rows[n] = rows
 
         load_tokens(0)
+        rope_raw = const.tile([P, PACK, ROPE], BF16)
+        for u in range(2):
+            nc.sync.dma_start(
+                out=rope_raw[:, 2 * u : 2 * u + 2, :], in_=wd_view[:, u, :, LATENT : LATENT + ROPE]
+            )
         wu_view = w_up.rearrange("(p j) n -> p j n", j=PACK)
         wu_raw = []
         for half in range(2):
@@ -85,19 +89,18 @@ def tile_multiheadlatentattention_pa_t_kernel(
         def regroup_latent_weights():
             nc.vector.tensor_copy(
                 out=wd_grouped[:, 0:LATENT, :].rearrange("p (t m) j -> p t m j", t=PACK),
-                in_=wd_raw[:, :, 0:LATENT].rearrange("p j (m t) -> p t m j", t=PACK),
+                in_=latent_raw[:].rearrange("p j (m t) -> p t m j", t=PACK),
             )
 
         def regroup_rope_weights():
-            rope_raw = wd_raw[:, :, LATENT : LATENT + ROPE]
             nc.scalar.copy(
                 out=wd_grouped[:, LATENT : LATENT + ROPE, :],
-                in_=rope_raw.rearrange("p j c -> p c j"),
+                in_=rope_raw[:].rearrange("p j c -> p c j"),
             )
             turned = wd_grouped[:, LATENT + ROPE : wd_cols, :].rearrange(
                 "p (q e) j -> p q e j", e=2
             )
-            rope_pairs = rope_raw.rearrange("p j (q e) -> p q e j", e=2)
+            rope_pairs = rope_raw[:].rearrange("p j (q e) -> p q e j", e=2)
             nc.scalar.mul(out=turned[:, :, 0, :], in_=rope_pairs[:, :, 1, :], mul=-1.0)
             nc.scalar.copy(out=turned[:, :, 1, :], in_=rope_pairs[:, :, 0, :])
 
@@ -272,8 +275,9 @@ def tile_multiheadlatentattention_pa_t_kernel(
                 if 0 <= g and 0 <= i < SIZES[g]:
                     if i % PAIR == 0:
                         open_pair(g, i)
-                        rope_pair(g, i)
                     up_slot(g, i)
+                    if i % PAIR == 0:
+                        rope_pair(g, i)
                     if i % PAIR == 1:
                         store_pair(g, i - 1)
                 if step == LEAD and 0 <= g + 2 < GROUPS:
@@ -282,9 +286,9 @@ def tile_multiheadlatentattention_pa_t_kernel(
                     quantise_latent(g + 1)
 
         regroup_latent_weights()
-        regroup_rope_weights()
         quantise_wkv_down(slice(0, LATENT))
         pipeline_round(-2)
+        regroup_rope_weights()
         regroup_w_up(0, nc.vector.tensor_copy)
         regroup_w_up(1, nc.scalar.copy)
         pipeline_round(-1)

@@ -32,7 +32,9 @@ LOAD_SLOTS = 4
 LOADS = ALL_SLOTS // LOAD_SLOTS
 WORDS = EMBED // 2
 BANK = 512
-STAGE_BUFS = 8
+STORED_K = (1,) * 8 + (2,) * 4
+STORED_V = (1,) * 12 + (2,) * 2
+STAGE_BUFS = 5
 LEAD = 1
 
 
@@ -192,9 +194,16 @@ def tile_multiheadlatentattention_pa_t_kernel(
             c_mx[g] = (codes, scales)
 
         def open_pair(g, i):
-            shape = [P, PAIR, HEADS, OUT_HEAD]
-            k_stage[g, i] = work.tile(shape, F32, tag="k_stage", name="k_stage", bufs=STAGE_BUFS)
-            v_stage[g, i] = work.tile(shape, F32, tag="v_stage", name="v_stage", bufs=STAGE_BUFS)
+            for stored, stage, tag in ((STORED_K, k_stage, "k_stage"), (STORED_V, v_stage, "v_stage")):
+                starts = [sum(stored[:n]) for n in range(len(stored))]
+                if g in starts:
+                    pairs = stored[starts.index(g)]
+                    rows = work.tile(
+                        [P, pairs * PAIR, HEADS, OUT_HEAD], F32, tag=tag, name=tag, bufs=STAGE_BUFS
+                    )
+                    for n in range(pairs):
+                        stage[g + n, i] = rows[:, n * PAIR : (n + 1) * PAIR, :, :]
+                    stage["store", g + pairs - 1] = (g, pairs, rows)
 
         def rope_pair(g, i):
             k_rows = k_stage[g, i]
@@ -259,11 +268,11 @@ def tile_multiheadlatentattention_pa_t_kernel(
         k_view = out_0.rearrange("b (p i) h d -> b p i h d", i=SLOTS_PER_ROW)
         v_view = out_1.rearrange("b (p i) h d -> b p i h d", i=SLOTS_PER_ROW)
 
-        def store_pair(g, i):
-            row, first = divmod(STARTS[g] + i, SLOTS_PER_ROW)
-            slots = slice(first, first + PAIR)
-            nc.sync.dma_start(out=v_view[row, :, slots, :, :], in_=v_stage[g, i][:])
-            nc.sync.dma_start(out=k_view[row, :, slots, :, :], in_=k_stage[g, i][:])
+        def store(view, stage, g):
+            if ("store", g) in stage:
+                start, pairs, rows = stage["store", g]
+                row, first = divmod(STARTS[start], SLOTS_PER_ROW)
+                nc.sync.dma_start(out=view[row, :, first : first + pairs * PAIR, :, :], in_=rows[:])
 
         def pipeline_round(g):
             if 0 <= g + 2 < GROUPS:
@@ -271,6 +280,9 @@ def tile_multiheadlatentattention_pa_t_kernel(
             for step in range(SLOTS + LEAD):
                 if 0 <= g + 1 < GROUPS and step < SIZES[g + 1]:
                     latent_slot(g + 1, step)
+                quantise_now = step == LEAD and 0 <= g + 2 < GROUPS
+                if quantise_now and g != 0:
+                    quantise_tokens(g + 2)
                 i = step - LEAD
                 if 0 <= g and 0 <= i < SIZES[g]:
                     if i % PAIR == 0:
@@ -279,8 +291,9 @@ def tile_multiheadlatentattention_pa_t_kernel(
                     if i % PAIR == 0:
                         rope_pair(g, i)
                     if i % PAIR == 1:
-                        store_pair(g, i - 1)
-                if step == LEAD and 0 <= g + 2 < GROUPS:
+                        store(v_view, v_stage, g)
+                        store(k_view, k_stage, g)
+                if quantise_now and g == 0:
                     quantise_tokens(g + 2)
                 if 0 <= g + 1 < GROUPS and step == SIZES[g + 1]:
                     quantise_latent(g + 1)

@@ -28,8 +28,8 @@ ALL_SLOTS = BATCH * SLOTS_PER_ROW
 SIZES = (SLOTS,) * (ALL_SLOTS // SLOTS)
 GROUPS = len(SIZES)
 STARTS = tuple(sum(SIZES[:g]) for g in range(GROUPS))
-LOAD_SLOTS = 4
-LOADS = ALL_SLOTS // LOAD_SLOTS
+LOAD_SLOTS = (PAIR, PAIR) + (4,) * (ALL_SLOTS // 4 - 1)
+LOAD_OF_SLOT = tuple((n, i) for n, slots in enumerate(LOAD_SLOTS) for i in range(slots))
 WORDS = EMBED // 2
 BANK = 512
 STORED_K = (1,) * 8 + (2,) * 4
@@ -49,35 +49,34 @@ def tile_multiheadlatentattention_pa_t_kernel(
         ctx.enter_context(tc.manual_schedule())
 
         wd_view = wkv_down.rearrange("(u p e) c -> p u e c", u=2, e=2)
-        latent_raw = const.tile([P, PACK, LATENT], BF16)
-        for u in range(2):
-            nc.sync.dma_start(out=latent_raw[:, 2 * u : 2 * u + 2, :], in_=wd_view[:, u, :, 0:LATENT])
+        wd_raw = const.tile([P, PACK, LATENT + ROPE], BF16)
+        nc.sync.dma_start(out=wd_raw[:].rearrange("p (u e) c -> p u e c", u=2), in_=wd_view)
+        latent_raw = wd_raw[:, :, 0:LATENT]
+        rope_raw = wd_raw[:, :, LATENT : LATENT + ROPE]
         x_view = x.rearrange("b (p i) k -> b p i k", i=SLOTS_PER_ROW)
         x_rows = {}
 
         def load_tokens(n):
-            row, first = divmod(n * LOAD_SLOTS, SLOTS_PER_ROW)
-            rows = const.tile([P, LOAD_SLOTS, EMBED], BF16, name="x_rows%d" % n)
-            nc.sync.dma_start(out=rows[:], in_=x_view[row, :, first : first + LOAD_SLOTS, :])
+            slots = LOAD_SLOTS[n]
+            row, first = divmod(LOAD_OF_SLOT.index((n, 0)), SLOTS_PER_ROW)
+            rows = const.tile([P, slots, EMBED], BF16, name="x_rows%d" % n)
+            nc.sync.dma_start(out=rows[:], in_=x_view[row, :, first : first + slots, :])
             x_rows[n] = rows
 
         load_tokens(0)
-        rope_raw = const.tile([P, PACK, ROPE], BF16)
-        for u in range(2):
-            nc.sync.dma_start(
-                out=rope_raw[:, 2 * u : 2 * u + 2, :], in_=wd_view[:, u, :, LATENT : LATENT + ROPE]
-            )
         wu_view = w_up.rearrange("(p j) n -> p j n", j=PACK)
         wu_raw = []
         for half in range(2):
             raw = const.tile([P, PACK, BANK], BF16, name="wu_raw%d" % half)
             nc.sync.dma_start(out=raw[:], in_=wu_view[:, :, half * BANK : (half + 1) * BANK])
             wu_raw.append(raw)
+            if half == 0:
+                load_tokens(1)
         cos_sb = const.tile([P, SLOTS_PER_ROW, ROPE // 2], BF16)
         nc.sync.dma_start(out=cos_sb[:], in_=cos.rearrange("(p i) j -> p i j", i=SLOTS_PER_ROW))
         sin_sb = const.tile([P, SLOTS_PER_ROW, ROPE // 2], BF16)
         nc.sync.dma_start(out=sin_sb[:], in_=sin.rearrange("(p i) j -> p i j", i=SLOTS_PER_ROW))
-        for n in range(1, LOADS):
+        for n in range(2, len(LOAD_SLOTS)):
             load_tokens(n)
 
         ident = const.tile([P, P], F32)
@@ -91,18 +90,18 @@ def tile_multiheadlatentattention_pa_t_kernel(
         def regroup_latent_weights():
             nc.vector.tensor_copy(
                 out=wd_grouped[:, 0:LATENT, :].rearrange("p (t m) j -> p t m j", t=PACK),
-                in_=latent_raw[:].rearrange("p j (m t) -> p t m j", t=PACK),
+                in_=latent_raw.rearrange("p j (m t) -> p t m j", t=PACK),
             )
 
         def regroup_rope_weights():
             nc.scalar.copy(
                 out=wd_grouped[:, LATENT : LATENT + ROPE, :],
-                in_=rope_raw[:].rearrange("p j c -> p c j"),
+                in_=rope_raw.rearrange("p j c -> p c j"),
             )
             turned = wd_grouped[:, LATENT + ROPE : wd_cols, :].rearrange(
                 "p (q e) j -> p q e j", e=2
             )
-            rope_pairs = rope_raw[:].rearrange("p j (q e) -> p q e j", e=2)
+            rope_pairs = rope_raw.rearrange("p j (q e) -> p q e j", e=2)
             nc.scalar.mul(out=turned[:, :, 0, :], in_=rope_pairs[:, :, 1, :], mul=-1.0)
             nc.scalar.copy(out=turned[:, :, 1, :], in_=rope_pairs[:, :, 0, :])
 
@@ -137,7 +136,7 @@ def tile_multiheadlatentattention_pa_t_kernel(
         v_stage = {}
 
         def transpose_tokens(g):
-            load, local = divmod(STARTS[g], LOAD_SLOTS)
+            load, local = LOAD_OF_SLOT[STARTS[g]]
             words = x_rows[load][:].rearrange("p i k -> p (i k)").bitcast(F32)
             grouped = work.tile([P, SIZES[g] * P * PACK], BF16, tag="x_grouped", align_bytes=64)
             grouped_words = grouped[:].bitcast(F32).rearrange("p (i n u) -> p i n u", n=P, u=2)

@@ -35,6 +35,7 @@ BANK = 512
 STORED_K = (1,) * 8 + (2,) * 4
 STORED_V = (1,) * 12 + (2,) * 2
 STAGE_BUFS = 5
+SECOND_SHARE = P
 LEAD = 1
 
 
@@ -72,11 +73,12 @@ def tile_multiheadlatentattention_pa_t_kernel(
             wu_raw.append(raw)
             if half == 0:
                 load_tokens(1)
+        load_tokens(2)
         cos_sb = const.tile([P, SLOTS_PER_ROW, ROPE // 2], BF16)
         nc.sync.dma_start(out=cos_sb[:], in_=cos.rearrange("(p i) j -> p i j", i=SLOTS_PER_ROW))
         sin_sb = const.tile([P, SLOTS_PER_ROW, ROPE // 2], BF16)
         nc.sync.dma_start(out=sin_sb[:], in_=sin.rearrange("(p i) j -> p i j", i=SLOTS_PER_ROW))
-        for n in range(2, len(LOAD_SLOTS)):
+        for n in range(3, len(LOAD_SLOTS)):
             load_tokens(n)
 
         ident = const.tile([P, P], F32)
@@ -116,9 +118,12 @@ def tile_multiheadlatentattention_pa_t_kernel(
         wu_codes = const.tile([P, HEADS * UP_HEAD], U32, align_bytes=64)
         wu_scales = const.tile([P, HEADS * UP_HEAD], U8, align_bytes=64)
 
-        def regroup_w_up(half, copy):
-            cols = slice(half * BANK, (half + 1) * BANK)
-            copy(out=wu_grouped[:, cols, :], in_=wu_raw[half][:].rearrange("p j c -> p c j"))
+        def regroup_w_up(half, first, last, copy):
+            cols = slice(half * BANK + first, half * BANK + last)
+            copy(
+                out=wu_grouped[:, cols, :],
+                in_=wu_raw[half][:, :, first:last].rearrange("p j c -> p c j"),
+            )
 
         def quantise_w_up(half):
             cols = slice(half * BANK, (half + 1) * BANK)
@@ -146,7 +151,7 @@ def tile_multiheadlatentattention_pa_t_kernel(
                     for u in range(2):
                         first = (local + i + s) * WORDS + u * P
                         nc.tensor.transpose(xt[:, s, u, :], words[:, first : first + P], ident[:])
-                copy = nc.scalar.copy if g % 2 == 0 else nc.vector.tensor_copy
+                copy = nc.scalar.copy if g % 2 == 0 or g == 1 else nc.vector.tensor_copy
                 copy(
                     out=grouped_words[:, i : i + PAIR, :, :],
                     in_=xt[:].rearrange("p s u n -> p s n u"),
@@ -301,9 +306,10 @@ def tile_multiheadlatentattention_pa_t_kernel(
         quantise_wkv_down(slice(0, LATENT))
         pipeline_round(-2)
         regroup_rope_weights()
-        regroup_w_up(0, nc.vector.tensor_copy)
-        regroup_w_up(1, nc.scalar.copy)
+        regroup_w_up(0, 0, BANK, nc.vector.tensor_copy)
         pipeline_round(-1)
+        regroup_w_up(1, 0, SECOND_SHARE, nc.vector.tensor_copy)
+        regroup_w_up(1, SECOND_SHARE, BANK, nc.scalar.copy)
         quantise_w_up(0)
         quantise_w_up(1)
         quantise_wkv_down(slice(LATENT, wd_cols))

from contextlib import ExitStack

import concourse.mybir as mybir
from concourse.masks import make_identity

F32 = mybir.dt.float32
BF16 = mybir.dt.bfloat16
U32 = mybir.dt.uint32
U8 = mybir.dt.uint8
FP8X4 = mybir.dt.float8_e4m3fn_x4
MULT = mybir.AluOpType.mult
ADD = mybir.AluOpType.add

P = 128
PACK = 4

BATCH, LENGTH, EMBED = 4, 1024, 512
HEADS, HEAD_DIM, LATENT, ROPE = 4, 64, 512, 128
UP_HEAD = 2 * HEAD_DIM + ROPE
OUT_HEAD = HEAD_DIM + ROPE

FLOPS = 2 * BATCH * LENGTH * (EMBED * (LATENT + ROPE) + LATENT * HEADS * UP_HEAD)

SLOTS_PER_ROW = LENGTH // P
PAIR = 2
SLOTS = 2
ALL_SLOTS = BATCH * SLOTS_PER_ROW
SIZES = (SLOTS,) * (ALL_SLOTS // SLOTS)
GROUPS = len(SIZES)
STARTS = tuple(sum(SIZES[:g]) for g in range(GROUPS))
LOAD_SLOTS = (PAIR, PAIR) + (4,) * (ALL_SLOTS // 4 - 1)
LOAD_OF_SLOT = tuple((n, i) for n, slots in enumerate(LOAD_SLOTS) for i in range(slots))
WORDS = EMBED // 2
BANK = 512
STORED_K = (1,) * 8 + (2,) * 4
STORED_V = (1,) * 12 + (2,) * 2
STAGE_BUFS = 5
SECOND_SHARE = P
LEAD = 1


def tile_multiheadlatentattention_pa_t_kernel(
    tc, x, cos, sin, wkv_down, w_up, out_0, out_1
):
    nc = tc.nc
    with ExitStack() as ctx:
        const = ctx.enter_context(tc.tile_pool(name="const", bufs=1))
        work = ctx.enter_context(tc.tile_pool(name="work", bufs=2))
        psum = ctx.enter_context(tc.psum_pool(name="psum", bufs=2))
        ctx.enter_context(tc.manual_schedule())

        wd_view = wkv_down.rearrange("(u p e) c -> p u e c", u=2, e=2)
        wd_raw = const.tile([P, PACK, LATENT + ROPE], BF16)
        nc.sync.dma_start(out=wd_raw[:].rearrange("p (u e) c -> p u e c", u=2), in_=wd_view)
        latent_raw = wd_raw[:, :, 0:LATENT]
        rope_raw = wd_raw[:, :, LATENT : LATENT + ROPE]
        x_view = x.rearrange("b (p i) k -> b p i k", i=SLOTS_PER_ROW)
        x_rows = {}

        def load_tokens(n):
            slots = LOAD_SLOTS[n]
            row, first = divmod(LOAD_OF_SLOT.index((n, 0)), SLOTS_PER_ROW)
            rows = const.tile([P, slots, EMBED], BF16, name="x_rows%d" % n)
            nc.sync.dma_start(out=rows[:], in_=x_view[row, :, first : first + slots, :])
            x_rows[n] = rows

        load_tokens(0)
        wu_view = w_up.rearrange("(p j) n -> p j n", j=PACK)
        wu_raw = []
        for half in range(2):
            raw = const.tile([P, PACK, BANK], BF16, name="wu_raw%d" % half)
            nc.sync.dma_start(out=raw[:], in_=wu_view[:, :, half * BANK : (half + 1) * BANK])
            wu_raw.append(raw)
            if half == 0:
                load_tokens(1)
        load_tokens(2)
        cos_sb = const.tile([P, SLOTS_PER_ROW, ROPE // 2], BF16)
        nc.sync.dma_start(out=cos_sb[:], in_=cos.rearrange("(p i) j -> p i j", i=SLOTS_PER_ROW))
        sin_sb = const.tile([P, SLOTS_PER_ROW, ROPE // 2], BF16)
        nc.sync.dma_start(out=sin_sb[:], in_=sin.rearrange("(p i) j -> p i j", i=SLOTS_PER_ROW))
        for n in range(3, len(LOAD_SLOTS)):
            load_tokens(n)

        ident = const.tile([P, P], F32)
        make_identity(nc, ident[:])

        wd_cols = LATENT + 2 * ROPE
        wd_grouped = const.tile([P, wd_cols, PACK], BF16, align_bytes=64)
        wd_codes = const.tile([P, wd_cols], U32, align_bytes=64)
        wd_scales = const.tile([P, wd_cols], U8, align_bytes=64)

        def regroup_latent_weights():
            nc.vector.tensor_copy(
                out=wd_grouped[:, 0:LATENT, :].rearrange("p (t m) j -> p t m j", t=PACK),
                in_=latent_raw.rearrange("p j (m t) -> p t m j", t=PACK),
            )

        def regroup_rope_weights():
            nc.scalar.copy(
                out=wd_grouped[:, LATENT : LATENT + ROPE, :],
                in_=rope_raw.rearrange("p j c -> p c j"),
            )
            turned = wd_grouped[:, LATENT + ROPE : wd_cols, :].rearrange(
                "p (q e) j -> p q e j", e=2
            )
            rope_pairs = rope_raw.rearrange("p j (q e) -> p q e j", e=2)
            nc.scalar.mul(out=turned[:, :, 0, :], in_=rope_pairs[:, :, 1, :], mul=-1.0)
            nc.scalar.copy(out=turned[:, :, 1, :], in_=rope_pairs[:, :, 0, :])

        def quantise_wkv_down(cols):
            nc.vector.quantize_mx(
                out=wd_codes[:, cols].bitcast(FP8X4),
                scales=wd_scales[:, cols],
                in_=wd_grouped[:, cols, :].rearrange("p c j -> p (c j)"),
            )

        wu_grouped = const.tile([P, HEADS * UP_HEAD, PACK], BF16, align_bytes=64)
        wu_codes = const.tile([P, HEADS * UP_HEAD], U32, align_bytes=64)
        wu_scales = const.tile([P, HEADS * UP_HEAD], U8, align_bytes=64)

        def regroup_w_up(half, first, last, copy):
            cols = slice(half * BANK + first, half * BANK + last)
            copy(
                out=wu_grouped[:, cols, :],
                in_=wu_raw[half][:, :, first:last].rearrange("p j c -> p c j"),
            )

        def quantise_w_up(half):
            cols = slice(half * BANK, (half + 1) * BANK)
            nc.vector.quantize_mx(
                out=wu_codes[:, cols].bitcast(FP8X4),
                scales=wu_scales[:, cols],
                in_=wu_grouped[:, cols, :].rearrange("p c j -> p (c j)"),
            )

        x_grouped = {}
        x_mx = {}
        c_grouped = {}
        c_mx = {}
        k_stage = {}
        v_stage = {}

        def transpose_tokens(g):
            load, local = LOAD_OF_SLOT[STARTS[g]]
            words = x_rows[load][:].rearrange("p i k -> p (i k)").bitcast(F32)
            grouped = work.tile([P, SIZES[g] * P * PACK], BF16, tag="x_grouped", align_bytes=64)
            grouped_words = grouped[:].bitcast(F32).rearrange("p (i n u) -> p i n u", n=P, u=2)
            for i in range(0, SIZES[g], PAIR):
                xt = psum.tile([P, PAIR, 2, P], F32, tag="xt", bufs=2)
                for s in range(PAIR):
                    for u in range(2):
                        first = (local + i + s) * WORDS + u * P
                        nc.tensor.transpose(xt[:, s, u, :], words[:, first : first + P], ident[:])
                copy = nc.scalar.copy if g % 2 == 0 or g == 1 else nc.vector.tensor_copy
                copy(
                    out=grouped_words[:, i : i + PAIR, :, :],
                    in_=xt[:].rearrange("p s u n -> p s n u"),
                )
            x_grouped[g] = grouped

        def quantise_tokens(g):
            codes = work.tile([P, SIZES[g] * P], U32, tag="x_codes", bufs=3, align_bytes=64)
            scales = work.tile([P, SIZES[g] * P], U8, tag="x_scales", bufs=3, align_bytes=64)
            nc.vector.quantize_mx(out=codes[:].bitcast(FP8X4), scales=scales[:], in_=x_grouped[g][:])
            x_mx[g] = (codes, scales)

        def latent_slot(g, i):
            if i == 0:
                c_grouped[g] = work.tile(
                    [P, SIZES[g] * P, PACK], BF16, tag="c_grouped", name="c_grouped", align_bytes=64
                )
            codes, scales = x_mx[g]
            tokens = slice(i * P, (i + 1) * P)
            c_ps = psum.tile([P, PACK, P], F32, tag="c", bufs=2)
            for t in range(PACK):
                block = slice(t * P, (t + 1) * P)
                nc.tensor.matmul_mx(
                    out=c_ps[:, t, :],
                    lhsT=wd_codes[:, block].bitcast(FP8X4),
                    lhsT_scale=wd_scales[:, block],
                    rhs=codes[:, tokens].bitcast(FP8X4),
                    rhs_scale=scales[:, tokens],
                    start=True,
                    stop=True,
                )
            nc.vector.tensor_copy(
                out=c_grouped[g][:, tokens, :], in_=c_ps[:].rearrange("p t n -> p n t")
            )

        def quantise_latent(g):
            codes = work.tile([P, SIZES[g] * P], U32, tag="c_codes", align_bytes=64)
            scales = work.tile([P, SIZES[g] * P], U8, tag="c_scales", align_bytes=64)
            nc.vector.quantize_mx(
                out=codes[:].bitcast(FP8X4),
                scales=scales[:],
                in_=c_grouped[g][:].rearrange("p n t -> p (n t)"),
            )
            c_mx[g] = (codes, scales)

        def open_pair(g, i):
            for stored, stage, tag in ((STORED_K, k_stage, "k_stage"), (STORED_V, v_stage, "v_stage")):
                starts = [sum(stored[:n]) for n in range(len(stored))]
                if g in starts:
                    pairs = stored[starts.index(g)]
                    rows = work.tile(
                        [P, pairs * PAIR, HEADS, OUT_HEAD], F32, tag=tag, name=tag, bufs=STAGE_BUFS
                    )
                    for n in range(pairs):
                        stage[g + n, i] = rows[:, n * PAIR : (n + 1) * PAIR, :, :]
                    stage["store", g + pairs - 1] = (g, pairs, rows)

        def rope_pair(g, i):
            k_rows = k_stage[g, i]
            codes, scales = x_mx[g]
            cols = slice(LATENT, wd_cols)
            r_ps = psum.tile([P, PAIR, 2, ROPE], F32, tag="r", bufs=1)
            for s in range(PAIR):
                tokens = slice((i + s) * P, (i + s + 1) * P)
                nc.tensor.matmul_mx(
                    out=r_ps[:, s, :, :].rearrange("p w c -> p (w c)"),
                    lhsT=codes[:, tokens].bitcast(FP8X4),
                    lhsT_scale=scales[:, tokens],
                    rhs=wd_codes[:, cols].bitcast(FP8X4),
                    rhs_scale=wd_scales[:, cols],
                    start=True,
                    stop=True,
                )
            first = STARTS[g] % SLOTS_PER_ROW + i
            terms = work.tile([P, 2, PAIR, ROPE], F32, tag="terms", bufs=3)
            for w, table in enumerate((cos_sb, sin_sb)):
                nc.vector.tensor_tensor(
                    out=terms[:, w, :, :].rearrange("p s (q e) -> p s q e", e=2),
                    in0=r_ps[:, :, w, :].rearrange("p s (q e) -> p s q e", e=2),
                    in1=table[:, first : first + PAIR, :]
                    .unsqueeze(3)
                    .to_broadcast([P, PAIR, ROPE // 2, 2]),
                    op=MULT,
                )
            nc.gpsimd.tensor_tensor(
                out=k_rows[:, :, 0, HEAD_DIM:OUT_HEAD], in0=terms[:, 0, :, :], in1=terms[:, 1, :, :], op=ADD
            )
            nc.gpsimd.tensor_scalar(
                out=k_rows[:, :, 1:HEADS, HEAD_DIM:OUT_HEAD],
                in0=k_rows[:, :, 0:1, HEAD_DIM:OUT_HEAD].to_broadcast([P, PAIR, HEADS - 1, ROPE]),
                scalar1=1.0,
                scalar2=0.0,
                op0=MULT,
                op1=ADD,
            )

        def up_slot(g, i):
            codes, scales = c_mx[g]
            tokens = slice(i * P, (i + 1) * P)
            k_rows = k_stage[g, i - i % PAIR]
            v_rows = v_stage[g, i - i % PAIR]
            for half in range(2):
                cols = slice(half * BANK, (half + 1) * BANK)
                heads = slice(2 * half, 2 * half + 2)
                up_ps = psum.tile([P, 2, UP_HEAD], F32, tag="up", bufs=3)
                nc.tensor.matmul_mx(
                    out=up_ps[:].rearrange("p h c -> p (h c)"),
                    lhsT=codes[:, tokens].bitcast(FP8X4),
                    lhsT_scale=scales[:, tokens],
                    rhs=wu_codes[:, cols].bitcast(FP8X4),
                    rhs_scale=wu_scales[:, cols],
                    start=True,
                    stop=True,
                )
                nc.scalar.copy(out=k_rows[:, i % PAIR, heads, 0:HEAD_DIM], in_=up_ps[:, :, 0:HEAD_DIM])
                nc.scalar.copy(out=v_rows[:, i % PAIR, heads, :], in_=up_ps[:, :, HEAD_DIM:UP_HEAD])

        k_view = out_0.rearrange("b (p i) h d -> b p i h d", i=SLOTS_PER_ROW)
        v_view = out_1.rearrange("b (p i) h d -> b p i h d", i=SLOTS_PER_ROW)

        def store(view, stage, g):
            if ("store", g) in stage:
                start, pairs, rows = stage["store", g]
                row, first = divmod(STARTS[start], SLOTS_PER_ROW)
                nc.sync.dma_start(out=view[row, :, first : first + pairs * PAIR, :, :], in_=rows[:])

        def pipeline_round(g):
            if 0 <= g + 2 < GROUPS:
                transpose_tokens(g + 2)
            for step in range(SLOTS + LEAD):
                if 0 <= g + 1 < GROUPS and step < SIZES[g + 1]:
                    latent_slot(g + 1, step)
                quantise_now = step == LEAD and 0 <= g + 2 < GROUPS
                if quantise_now and g != 0:
                    quantise_tokens(g + 2)
                i = step - LEAD
                if 0 <= g and 0 <= i < SIZES[g]:
                    if i % PAIR == 0:
                        open_pair(g, i)
                    up_slot(g, i)
                    if i % PAIR == 0:
                        rope_pair(g, i)
                    if i % PAIR == 1:
                        store(v_view, v_stage, g)
                        store(k_view, k_stage, g)
                if quantise_now and g == 0:
                    quantise_tokens(g + 2)
                if 0 <= g + 1 < GROUPS and step == SIZES[g + 1]:
                    quantise_latent(g + 1)

        regroup_latent_weights()
        quantise_wkv_down(slice(0, LATENT))
        pipeline_round(-2)
        regroup_rope_weights()
        regroup_w_up(0, 0, BANK, nc.vector.tensor_copy)
        pipeline_round(-1)
        regroup_w_up(1, 0, SECOND_SHARE, nc.vector.tensor_copy)
        regroup_w_up(1, SECOND_SHARE, BANK, nc.scalar.copy)
        quantise_w_up(0)
        quantise_w_up(1)
        quantise_wkv_down(slice(LATENT, wd_cols))
        for g in range(GROUPS):
            pipeline_round(g)
